import numpy as np
import ml_dtypes


def mxq(x, axis, fmt="e4m3"):
    dtype, down = {"e4m3": (ml_dtypes.float8_e4m3fn, 7), "e5m2": (ml_dtypes.float8_e5m2, 14)}[fmt]
    v = np.moveaxis(np.asarray(x, np.float32).astype(ml_dtypes.bfloat16).astype(np.float64), axis, -1)
    blocks = v.reshape(v.shape[:-1] + (-1, 32))
    amax = np.abs(blocks).max(-1, keepdims=True)
    byte = np.maximum(np.where(amax > 0, np.frexp(amax)[1] - 1 + 127, 0) - down, 1)
    scale = np.exp2(byte - 127.0)
    codes = (blocks / scale).astype(np.float32).astype(dtype).astype(np.float64)
    return np.moveaxis((codes * scale).reshape(v.shape), -1, axis)


WIDE = False


def mx_kscale(k):
    if not WIDE:
        return np.ones(k)
    levels = np.array([10, -10, 5, -5, 0])
    if k % 512:
        return np.exp2(np.random.permutation(np.resize(levels, k // 32))).repeat(32)
    a = np.empty((k // 512, 16))
    for p in range(k // 512):
        a[p, :8] = np.random.permutation(np.resize(levels, 8))
        for g in range(8):
            far = levels[np.abs(levels - a[p, g]) >= 10]
            a[p, g + 8] = far[np.random.randint(len(far))]
    return np.exp2(a.ravel()).repeat(32)


BF16 = ml_dtypes.bfloat16


def bf(x):
    return np.asarray(x, np.float32).astype(BF16)


def f64(x):
    return np.asarray(x).astype(np.float64)


B, DIM, D_IN, HID = 8192, 256, 128, 512
D_OUT = DIM - D_IN
LOG_SCALE_CLAMP = 2.0


def _net_draw(c_out):
    k, f = mx_kscale(HID), mx_kscale(HID)
    h = bf(np.maximum(np.random.standard_normal((B, HID)), 0.0) * np.sqrt(2.0) * k)
    w_hid = bf(np.random.standard_normal((HID, HID)) * np.sqrt(2.0 / HID) * f[:, None] / k[None, :])
    b_hid = bf(np.random.standard_normal(HID) * 0.3 * f)
    w_out = bf(np.random.standard_normal((D_OUT, HID)) * c_out / np.sqrt(HID) / f[None, :])
    b_out = bf(np.random.standard_normal(D_OUT) * 0.3)
    return h, w_hid, b_hid, w_out, b_out


def setup_inputs():
    z = bf(np.random.standard_normal((B, DIM)))
    h_s, s_Whid1, s_bhid1, s_Wout, s_bout = _net_draw(1.2)
    h_t, t_Whid1, t_bhid1, t_Wout, t_bout = _net_draw(1.0)
    return {"z": z, "h_s": h_s, "h_t": h_t,
            "s_Whid1": s_Whid1, "s_bhid1": s_bhid1, "s_Wout": s_Wout, "s_bout": s_bout,
            "t_Whid1": t_Whid1, "t_bhid1": t_bhid1, "t_Wout": t_Wout, "t_bout": t_bout}


def _tail(h, w_hid, b_hid, w_out, b_out):
    g = np.maximum((mxq(f64(h), 1, "e4m3") @ mxq(f64(w_hid), 1, "e4m3").T) + f64(b_hid), 0.0)
    return (mxq(g, 1, "e4m3") @ mxq(f64(w_out), 1, "e4m3").T) + f64(b_out)


def reference(z, h_s, h_t, s_Whid1, s_bhid1, s_Wout, s_bout, t_Whid1, t_bhid1, t_Wout, t_bout):
    z = f64(z)
    z1 = z[:, :D_IN]
    z2 = z[:, D_IN:]
    log_s = np.clip(_tail(h_s, s_Whid1, s_bhid1, s_Wout, s_bout), -LOG_SCALE_CLAMP, LOG_SCALE_CLAMP)
    t = _tail(h_t, t_Whid1, t_bhid1, t_Wout, t_bout)
    z2_out = z2 * np.exp(log_s) + t
    z_out = np.concatenate([z1, z2_out], axis=1)
    log_det = log_s.sum(axis=-1)
    return (z_out, log_det)

@@ -1,0 +1,319 @@
+from contextlib import ExitStack
+
+import concourse.mybir as mybir
+from concourse.masks import make_identity
+
+F32 = mybir.dt.float32
+BF16 = mybir.dt.bfloat16
+U32 = mybir.dt.uint32
+U8 = mybir.dt.uint8
+FP8X4 = mybir.dt.float8_e4m3fn_x4
+ACT = mybir.ActivationFunctionType
+ALU = mybir.AluOpType
+AX = mybir.AxisListType
+
+P = 128
+B, DIM, HID, D_OUT = 8192, 256, 512, 128
+PACK = 4
+ROWS_PP = B // P
+TILES = 4
+COLS = TILES * P
+LOAD_TILES = 8
+N_CHUNKS = ROWS_PP // TILES
+N_UNITS = 2 * N_CHUNKS
+N_LOADS = ROWS_PP // LOAD_TILES
+WORDS = HID // 2
+FLOPS = 2 * 2 * B * HID * (HID + D_OUT)
+
+
+def tile_affinecouplinglayer_pa_t_kernel(
+    tc, z, h_s, h_t, s_Whid1, s_bhid1, s_Wout, s_bout, t_Whid1, t_bhid1, t_Wout, t_bout, out_0, out_1
+):
+    nc = tc.nc
+    h_in = (h_s.rearrange("(p i) k -> p i k", i=ROWS_PP), h_t.rearrange("(p i) k -> p i k", i=ROWS_PP))
+    z_in = z.rearrange("(p i) d -> p i d", i=ROWS_PP)
+    z_out = out_0.rearrange("(p i) d -> p i d", i=ROWS_PP)
+    w_hid = (s_Whid1, t_Whid1)
+    b_hid = (s_bhid1, t_bhid1)
+    w_out = (s_Wout, t_Wout)
+    b_out = (s_bout, t_bout)
+
+    with ExitStack() as ctx:
+        const = ctx.enter_context(tc.tile_pool(name="const", bufs=1))
+        hpool = ctx.enter_context(tc.tile_pool(name="hpool", bufs=3))
+        zpool = ctx.enter_context(tc.tile_pool(name="zpool", bufs=5))
+        ring2 = ctx.enter_context(tc.tile_pool(name="ring2", bufs=2))
+        ring3 = ctx.enter_context(tc.tile_pool(name="ring3", bufs=3))
+        ring4 = ctx.enter_context(tc.tile_pool(name="ring4", bufs=4))
+        gate = ctx.enter_context(tc.tile_pool(name="gate", bufs=1))
+        tp_pool = ctx.enter_context(tc.psum_pool(name="tp_pool", bufs=2))
+        m1_pool = ctx.enter_context(tc.psum_pool(name="m1_pool", bufs=4))
+        m2_pool = ctx.enter_context(tc.psum_pool(name="m2_pool", bufs=2))
+        ctx.enter_context(tc.manual_schedule())
+
+        h_sb, z_sb = {}, {}
+        w_sb, wo_sb, bh_raw, bo_raw = [], [], [], []
+
+        def load_h_rows(n, s, i0, i1):
+            nc.sync.dma_start(
+                out=h_sb[(n, s)][:, i0 * HID : i1 * HID].rearrange("p (i k) -> p i k", k=HID),
+                in_=h_in[n][:, s * LOAD_TILES + i0 : s * LOAD_TILES + i1, :],
+            )
+
+        def new_h(n, s):
+            t = hpool.tile([P, LOAD_TILES * HID], BF16, name="h%d" % n)
+            h_sb[(n, s)] = t
+
+        def load(s):
+            for n in range(2):
+                new_h(n, s)
+                load_h_rows(n, s, 0, LOAD_TILES)
+            t = zpool.tile([P, LOAD_TILES, DIM], BF16, name="zt")
+            z_sb[s] = t
+            nc.sync.dma_start(out=t[:], in_=z_in[:, s * LOAD_TILES : (s + 1) * LOAD_TILES, :])
+
+        for n in range(2):
+            wt = const.tile([P, PACK * HID], BF16, name="w_sb%d" % n)
+            nc.sync.dma_start(out=wt[:], in_=w_hid[n].rearrange("(p t) k -> p (t k)", t=PACK))
+            w_sb.append(wt)
+            new_h(n, 0)
+            load_h_rows(n, 0, 0, TILES)
+            br = const.tile([P, PACK], BF16, name="bh_raw%d" % n)
+            nc.scalar.dma_start(out=br[:], in_=b_hid[n].rearrange("(p t) -> p t", t=PACK))
+            bh_raw.append(br)
+            wo = const.tile([P, HID], BF16, name="wo_sb%d" % n)
+            nc.scalar.dma_start(out=wo[:], in_=w_out[n])
+            wo_sb.append(wo)
+        for n in range(2):
+            bo = const.tile([P, D_OUT], BF16, name="bo_raw%d" % n)
+            nc.scalar.dma_start(out=bo[:], in_=b_out[n].partition_broadcast(P))
+            bo_raw.append(bo)
+        for n in range(2):
+            load_h_rows(n, 0, TILES, LOAD_TILES)
+        z0 = zpool.tile([P, LOAD_TILES, DIM], BF16, name="zt")
+        z_sb[0] = z0
+        nc.sync.dma_start(out=z0[:], in_=z_in[:, 0:LOAD_TILES, :])
+        load(1)
+
+        ident = const.tile([P, P], F32, name="ident")
+        make_identity(nc, ident[:])
+
+        def to_k_major(words, first_word, grouped_words, weights):
+            for half in range(2):
+                if weights:
+                    bank = m1_pool.tile([P, 2, 2 * P], F32, name="m1")
+                else:
+                    bank = tp_pool.tile([P, 2, 2 * P], F32, name="tp")
+                for r in range(2):
+                    for u in range(2):
+                        w0 = first_word + (2 * half + r) * WORDS
+                        nc.tensor.transpose(bank[:, u, r * P : (r + 1) * P], words[:, w0 + u : w0 + WORDS : 2], ident[:])
+                dst = grouped_words[:, half * 4 * P : (half + 1) * 4 * P].rearrange("p (b u) -> p b u", u=2)
+                src = bank[:].rearrange("p u b -> p b u")
+                if weights:
+                    nc.vector.tensor_copy(out=dst, in_=src)
+                else:
+                    nc.scalar.copy(out=dst, in_=src)
+
+        wc, wsc, woc, wosc, bh, bo = [], [], [], [], [], []
+
+        def prep_w(n):
+            wq = const.tile([P, PACK * HID], BF16, name="wq%d" % n, align_bytes=64)
+            to_k_major(w_sb[n][:].bitcast(F32), 0, wq[:].bitcast(F32), True)
+            c = const.tile([P, HID], U32, name="wc%d" % n, align_bytes=64)
+            s = const.tile([P, HID], U8, name="wsc%d" % n, align_bytes=64)
+            nc.vector.quantize_mx(out=c[:].bitcast(FP8X4), scales=s[:], in_=wq[:])
+            wc.append(c)
+            wsc.append(s)
+            b32 = const.tile([P, PACK], F32, name="bh%d" % n)
+            nc.vector.tensor_copy(out=b32[:], in_=bh_raw[n][:])
+            bh.append(b32)
+
+        def prep_wout(n):
+            bank = m2_pool.tile([P, 2, 2 * P], F32, name="m2")
+            wv = wo_sb[n][:].bitcast(F32).rearrange("p (q u) -> p u q", u=2)
+            for u in range(2):
+                nc.tensor.transpose(bank[:, u, 0:P], wv[:, u, :], ident[:])
+            woq = const.tile([P, PACK * D_OUT], BF16, name="woq%d" % n, align_bytes=64)
+            nc.vector.tensor_copy(
+                out=woq[:].bitcast(F32).rearrange("p (b u) -> p b u", u=2),
+                in_=bank[:, :, 0:P].rearrange("p u b -> p b u"),
+            )
+            c = const.tile([P, D_OUT], U32, name="woc%d" % n, align_bytes=64)
+            s = const.tile([P, D_OUT], U8, name="wosc%d" % n, align_bytes=64)
+            nc.vector.quantize_mx(out=c[:].bitcast(FP8X4), scales=s[:], in_=woq[:])
+            woc.append(c)
+            wosc.append(s)
+            b32 = const.tile([P, D_OUT], F32, name="bo%d" % n)
+            nc.vector.tensor_copy(out=b32[:], in_=bo_raw[n][:])
+            bo.append(b32)
+
+        log_det = const.tile([P, ROWS_PP], F32, name="log_det")
+
+        hq, hc, hsc, gt, gg, gc, gsc, o_ps = {}, {}, {}, {}, {}, {}, {}, {}
+        ls_t, ex_t, ot_t, sh_t, mz_t = {}, {}, {}, {}, {}
+
+        def transpose_h(u):
+            c, n = u // 2, u % 2
+            if n == 0:
+                t = ring3.tile([P, 2 * PACK * COLS], BF16, name="hq", align_bytes=64)
+                hq[c] = t
+            to_k_major(
+                h_sb[(n, c // 2)][:].bitcast(F32),
+                (c % 2) * TILES * WORDS,
+                hq[c][:].bitcast(F32)[:, n * 2 * COLS : (n + 1) * 2 * COLS],
+                False,
+            )
+
+        def quantise_h(c, n0, n1):
+            if n0 == 0:
+                cw = ring3.tile([P, 2 * COLS], U32, name="hc", align_bytes=64)
+                sw = ring3.tile([P, 2 * COLS], U8, name="hsc", align_bytes=64)
+                hc[c], hsc[c] = cw, sw
+            nc.vector.quantize_mx(
+                out=hc[c][:, n0 * COLS : n1 * COLS].bitcast(FP8X4),
+                scales=hsc[c][:, n0 * COLS : n1 * COLS],
+                in_=hq[c][:, n0 * PACK * COLS : n1 * PACK * COLS],
+            )
+
+        def hidden_layer(u):
+            c, n = u // 2, u % 2
+            if n == 0:
+                g = ring3.tile([P, PACK, 2 * COLS], BF16, name="gt")
+                gt[c] = g
+            cols = slice(n * COLS, (n + 1) * COLS)
+            for t in range(PACK):
+                acc = m1_pool.tile([P, COLS], F32, name="m1")
+                nc.tensor.matmul_mx(
+                    out=acc[:],
+                    lhsT=wc[n][:, t * P : (t + 1) * P].bitcast(FP8X4),
+                    lhsT_scale=wsc[n][:, t * P : (t + 1) * P],
+                    rhs=hc[c][:, cols].bitcast(FP8X4),
+                    rhs_scale=hsc[c][:, cols],
+                    start=True,
+                    stop=True,
+                )
+                nc.scalar.activation(out=gt[c][:, t, cols], in_=acc[:], func=ACT.Relu, bias=bh[n][:, t : t + 1], scale=1.0)
+
+        def regroup_g(c):
+            t = ring2.tile([P, 2 * COLS, PACK], BF16, name="gg", align_bytes=64)
+            gg[c] = t
+            nc.vector.tensor_copy(
+                out=t[:].rearrange("p (c i) t -> p c t i", i=4),
+                in_=gt[c][:].rearrange("p t (c i) -> p c t i", i=4),
+            )
+
+        def quantise_g(c):
+            cw = ring2.tile([P, 2 * COLS], U32, name="gc", align_bytes=64)
+            sw = ring2.tile([P, 2 * COLS], U8, name="gsc", align_bytes=64)
+            nc.vector.quantize_mx(out=cw[:].bitcast(FP8X4), scales=sw[:], in_=gg[c][:].rearrange("p b t -> p (b t)"))
+            gc[c], gsc[c] = cw, sw
+
+        def output_layer(c):
+            for n in range(2):
+                o = m2_pool.tile([P, TILES, D_OUT], F32, name="m2")
+                o_ps[(c, n)] = o
+                for r in range(TILES):
+                    cols = slice(n * COLS + r * P, n * COLS + (r + 1) * P)
+                    nc.tensor.matmul_mx(
+                        out=o[:, r, :],
+                        lhsT=gc[c][:, cols].bitcast(FP8X4),
+                        lhsT_scale=gsc[c][:, cols],
+                        rhs=woc[n][:].bitcast(FP8X4),
+                        rhs_scale=wosc[n][:],
+                        start=True,
+                        stop=True,
+                    )
+
+        def bias_rows(n):
+            return bo[n][:].unsqueeze(1).to_broadcast([P, TILES, D_OUT])
+
+        def z_rows(c, lo):
+            i0 = (c % 2) * TILES
+            return z_sb[c // 2][:, i0 : i0 + TILES, lo : lo + D_OUT]
+
+        def add_scale_bias(c):
+            ls = ring3.tile([P, TILES, D_OUT], F32, name="ls")
+            ls_t[c] = ls
+            nc.vector.tensor_tensor(out=ls[:], in0=o_ps[(c, 0)][:], in1=bias_rows(0), op=ALU.add)
+
+        def add_shift_bias(c):
+            sh = ring3.tile([P, TILES, D_OUT], F32, name="sh")
+            sh_t[c] = sh
+            nc.vector.tensor_tensor(out=sh[:], in0=o_ps[(c, 1)][:], in1=bias_rows(1), op=ALU.add)
+
+        def clamp(c):
+            ls = ls_t[c]
+            nc.vector.tensor_scalar(out=ls[:], in0=ls[:], scalar1=-2.0, scalar2=2.0, op0=ALU.max, op1=ALU.min)
+
+        def exponential(c):
+            ex = ring2.tile([P, TILES, D_OUT], F32, name="ex")
+            ex_t[c] = ex
+            nc.scalar.activation(out=ex[:], in_=ls_t[c][:], func=ACT.Exp)
+
+        def row_sums(c):
+            nc.vector.tensor_reduce(out=log_det[:, c * TILES : (c + 1) * TILES], in_=ls_t[c][:], axis=AX.X, op=ALU.add)
+
+        def scale_z2(c):
+            mz = gate.tile([P, TILES, D_OUT], F32, name="mz")
+            mz_t[c] = mz
+            nc.gpsimd.tensor_tensor(out=mz[:], in0=z_rows(c, D_OUT), in1=ex_t[c][:], op=ALU.mult)
+
+        def cast_z1_first_half(c):
+            ot = ring4.tile([P, TILES, DIM], F32, name="ot")
+            ot_t[c] = ot
+            nc.gpsimd.tensor_scalar(
+                out=ot[:, 0 : TILES // 2, 0:D_OUT],
+                in0=z_rows(c, 0)[:, 0 : TILES // 2, :],
+                scalar1=1.0,
+                scalar2=0.0,
+                op0=ALU.mult,
+                op1=ALU.add,
+            )
+
+        def cast_z1_second_half(c):
+            nc.scalar.copy(out=ot_t[c][:, TILES // 2 : TILES, 0:D_OUT], in_=z_rows(c, 0)[:, TILES // 2 : TILES, :])
+
+        def finish(c):
+            nc.vector.tensor_tensor(out=ot_t[c][:, :, D_OUT:DIM], in0=mz_t[c][:], in1=sh_t[c][:], op=ALU.add)
+            nc.sync.dma_start(out=z_out[:, c * TILES : (c + 1) * TILES, :], in_=ot_t[c][:])
+
+        def when(it, first, fn):
+            c = (it - first) // 2
+            if it >= first and (it - first) % 2 == 0 and c < N_CHUNKS:
+                fn(c)
+
+        prep_w(0)
+        transpose_h(0)
+        quantise_h(0, 0, 1)
+        prep_w(1)
+        transpose_h(1)
+
+        for it in range(N_UNITS + 8):
+            when(it, 7, exponential)
+            if it < N_UNITS:
+                hidden_layer(it)
+            if it == 0:
+                prep_wout(0)
+                prep_wout(1)
+                transpose_h(2)
+            if it + 3 < N_UNITS:
+                if (it + 3) % 4 == 0 and (it + 3) // 4 + 1 < N_LOADS:
+                    load((it + 3) // 4 + 1)
+                transpose_h(it + 3)
+            when(it, 4, output_layer)
+            when(it, 8, cast_z1_second_half)
+            if it == 0:
+                quantise_h(0, 1, 2)
+            if it % 2 == 1 and (it + 1) // 2 < N_CHUNKS:
+                quantise_h((it + 1) // 2, 0, 2)
+            when(it, 9, finish)
+            when(it, 7, scale_z2)
+            when(it, 7, cast_z1_first_half)
+            when(it, 5, add_scale_bias)
+            when(it, 5, add_shift_bias)
+            when(it, 7, row_sums)
+            when(it, 2, regroup_g)
+            when(it, 6, clamp)
+            when(it, 2, quantise_g)
+        nc.sync.dma_start(out=out_1.rearrange("(p i) -> p i", i=ROWS_PP), in_=log_det[:])

@@ -98,7 +98,8 @@ def tile_affinecouplinglayer_pa_t_kernel(
         ident = const.tile([P, P], F32, name="ident")
         make_identity(nc, ident[:])
 
-        def to_k_major(words, first_word, grouped_words, weights):
+        def to_k_major(words, first_word, grouped_words, weights, vector_half):
+            later = []
             for half in range(2):
                 if weights:
                     bank = m1_pool.tile([P, 2, 2 * P], F32, name="m1")
@@ -112,14 +113,17 @@ def tile_affinecouplinglayer_pa_t_kernel(
                 src = bank[:].rearrange("p u b -> p b u")
                 if weights:
                     nc.vector.tensor_copy(out=dst, in_=src)
+                elif half == vector_half:
+                    later.append((dst, src))
                 else:
                     nc.scalar.copy(out=dst, in_=src)
+            return later
 
         wc, wsc, woc, wosc, bh, bo = [], [], [], [], [], []
 
         def prep_w(n):
             wq = const.tile([P, PACK * HID], BF16, name="wq%d" % n, align_bytes=64)
-            to_k_major(w_sb[n][:].bitcast(F32), 0, wq[:].bitcast(F32), True)
+            to_k_major(w_sb[n][:].bitcast(F32), 0, wq[:].bitcast(F32), True, None)
             c = const.tile([P, HID], U32, name="wc%d" % n, align_bytes=64)
             s = const.tile([P, HID], U8, name="wsc%d" % n, align_bytes=64)
             nc.vector.quantize_mx(out=c[:].bitcast(FP8X4), scales=s[:], in_=wq[:])
@@ -153,16 +157,17 @@ def tile_affinecouplinglayer_pa_t_kernel(
         hq, hc, hsc, gt, gg, gc, gsc, o_ps = {}, {}, {}, {}, {}, {}, {}, {}
         ls_t, ex_t, ot_t, sh_t, mz_t = {}, {}, {}, {}, {}
 
-        def transpose_h(u):
+        def transpose_h(u, vector_half=None):
             c, n = u // 2, u % 2
             if n == 0:
                 t = ring3.tile([P, 2 * PACK * COLS], BF16, name="hq", align_bytes=64)
                 hq[c] = t
-            to_k_major(
+            return to_k_major(
                 h_sb[(n, c // 2)][:].bitcast(F32),
                 (c % 2) * TILES * WORDS,
                 hq[c][:].bitcast(F32)[:, n * 2 * COLS : (n + 1) * 2 * COLS],
                 False,
+                vector_half,
             )
 
         def quantise_h(c, n0, n1):
@@ -290,6 +295,7 @@ def tile_affinecouplinglayer_pa_t_kernel(
         transpose_h(1)
 
         for it in range(N_UNITS + 8):
+            vector_copies = []
             when(it, 7, exponential)
             if it < N_UNITS:
                 hidden_layer(it)
@@ -300,7 +306,7 @@ def tile_affinecouplinglayer_pa_t_kernel(
             if it + 3 < N_UNITS:
                 if (it + 3) % 4 == 0 and (it + 3) // 4 + 1 < N_LOADS:
                     load((it + 3) // 4 + 1)
-                transpose_h(it + 3)
+                vector_copies = transpose_h(it + 3, 1 if it % 2 == 1 else None)
             when(it, 4, output_layer)
             when(it, 8, cast_z1_second_half)
             if it == 0:
@@ -312,6 +318,8 @@ def tile_affinecouplinglayer_pa_t_kernel(
             when(it, 7, cast_z1_first_half)
             when(it, 5, add_scale_bias)
             when(it, 5, add_shift_bias)
+            for dst, src in vector_copies:
+                nc.vector.tensor_copy(out=dst, in_=src)
             when(it, 7, row_sums)
             when(it, 2, regroup_g)
             when(it, 6, clamp)

@@ -264,20 +264,17 @@ def tile_affinecouplinglayer_pa_t_kernel(
             mz_t[c] = mz
             nc.gpsimd.tensor_tensor(out=mz[:], in0=z_rows(c, D_OUT), in1=ex_t[c][:], op=ALU.mult)
 
-        def cast_z1_first_half(c):
+        def cast_z1(c):
             ot = ring4.tile([P, TILES, DIM], F32, name="ot")
             ot_t[c] = ot
             nc.gpsimd.tensor_scalar(
-                out=ot[:, 0 : TILES // 2, 0:D_OUT],
-                in0=z_rows(c, 0)[:, 0 : TILES // 2, :],
+                out=ot[:, :, 0:D_OUT],
+                in0=z_rows(c, 0),
                 scalar1=1.0,
                 scalar2=0.0,
                 op0=ALU.mult,
                 op1=ALU.add,
             )
-
-        def cast_z1_second_half(c):
-            nc.scalar.copy(out=ot_t[c][:, TILES // 2 : TILES, 0:D_OUT], in_=z_rows(c, 0)[:, TILES // 2 : TILES, :])
 
         def finish(c):
             nc.vector.tensor_tensor(out=ot_t[c][:, :, D_OUT:DIM], in0=mz_t[c][:], in1=sh_t[c][:], op=ALU.add)
@@ -306,16 +303,15 @@ def tile_affinecouplinglayer_pa_t_kernel(
             if it + 3 < N_UNITS:
                 if (it + 3) % 4 == 0 and (it + 3) // 4 + 1 < N_LOADS:
                     load((it + 3) // 4 + 1)
-                vector_copies = transpose_h(it + 3, 1 if it % 2 == 1 else None)
+                vector_copies = transpose_h(it + 3, 1 if it % 4 == 1 else None)
             when(it, 4, output_layer)
-            when(it, 8, cast_z1_second_half)
             if it == 0:
                 quantise_h(0, 1, 2)
             if it % 2 == 1 and (it + 1) // 2 < N_CHUNKS:
                 quantise_h((it + 1) // 2, 0, 2)
             when(it, 9, finish)
             when(it, 7, scale_z2)
-            when(it, 7, cast_z1_first_half)
+            when(it, 7, cast_z1)
             when(it, 5, add_scale_bias)
             when(it, 5, add_shift_bias)
             for dst, src in vector_copies:

@@ -45,14 +45,15 @@ def tile_affinecouplinglayer_pa_t_kernel(
         ring2 = ctx.enter_context(tc.tile_pool(name="ring2", bufs=2))
         ring3 = ctx.enter_context(tc.tile_pool(name="ring3", bufs=3))
         ring4 = ctx.enter_context(tc.tile_pool(name="ring4", bufs=4))
-        gate = ctx.enter_context(tc.tile_pool(name="gate", bufs=1))
+        gate = ctx.enter_context(tc.tile_pool(name="gate", bufs=2))
         tp_pool = ctx.enter_context(tc.psum_pool(name="tp_pool", bufs=2))
         m1_pool = ctx.enter_context(tc.psum_pool(name="m1_pool", bufs=4))
-        m2_pool = ctx.enter_context(tc.psum_pool(name="m2_pool", bufs=2))
+        os_pool = ctx.enter_context(tc.psum_pool(name="os_pool", bufs=1))
+        ot_pool = ctx.enter_context(tc.psum_pool(name="ot_pool", bufs=1))
         ctx.enter_context(tc.manual_schedule())
 
         h_sb, z_sb = {}, {}
-        w_sb, wo_sb, bh_raw, bo_raw = [], [], [], []
+        w_sb, wo_sb, bh_raw = [], [], []
 
         def load_h_rows(n, s, i0, i1):
             nc.sync.dma_start(
@@ -84,10 +85,10 @@ def tile_affinecouplinglayer_pa_t_kernel(
             wo = const.tile([P, HID], BF16, name="wo_sb%d" % n)
             nc.scalar.dma_start(out=wo[:], in_=w_out[n])
             wo_sb.append(wo)
-        for n in range(2):
-            bo = const.tile([P, D_OUT], BF16, name="bo_raw%d" % n)
-            nc.scalar.dma_start(out=bo[:], in_=b_out[n].partition_broadcast(P))
-            bo_raw.append(bo)
+        bo_s_raw = const.tile([P, D_OUT], BF16, name="bo_s_raw")
+        nc.scalar.dma_start(out=bo_s_raw[:], in_=b_out[0].partition_broadcast(P))
+        bo_t_raw = const.tile([P, 1], BF16, name="bo_t_raw")
+        nc.scalar.dma_start(out=bo_t_raw[:], in_=b_out[1].rearrange("(p o) -> p o", o=1))
         for n in range(2):
             load_h_rows(n, 0, TILES, LOAD_TILES)
         z0 = zpool.tile([P, LOAD_TILES, DIM], BF16, name="zt")
@@ -119,7 +120,7 @@ def tile_affinecouplinglayer_pa_t_kernel(
                     nc.scalar.copy(out=dst, in_=src)
             return later
 
-        wc, wsc, woc, wosc, bh, bo = [], [], [], [], [], []
+        wc, wsc, woc, wosc, bh = [], [], [], [], []
 
         def prep_w(n):
             wq = const.tile([P, PACK * HID], BF16, name="wq%d" % n, align_bytes=64)
@@ -134,7 +135,10 @@ def tile_affinecouplinglayer_pa_t_kernel(
             bh.append(b32)
 
         def prep_wout(n):
-            bank = m2_pool.tile([P, 2, 2 * P], F32, name="m2")
+            if n == 0:
+                bank = os_pool.tile([P, 2, 2 * P], F32, name="os")
+            else:
+                bank = ot_pool.tile([P, 2, 2 * P], F32, name="ot_ps")
             wv = wo_sb[n][:].bitcast(F32).rearrange("p (q u) -> p u q", u=2)
             for u in range(2):
                 nc.tensor.transpose(bank[:, u, 0:P], wv[:, u, :], ident[:])
@@ -148,13 +152,17 @@ def tile_affinecouplinglayer_pa_t_kernel(
             nc.vector.quantize_mx(out=c[:].bitcast(FP8X4), scales=s[:], in_=woq[:])
             woc.append(c)
             wosc.append(s)
-            b32 = const.tile([P, D_OUT], F32, name="bo%d" % n)
-            nc.vector.tensor_copy(out=b32[:], in_=bo_raw[n][:])
-            bo.append(b32)
+
+        bo_s = const.tile([P, D_OUT], F32, name="bo_s")
+        bo_t = const.tile([P, 1], F32, name="bo_t")
+
+        def prep_bout():
+            nc.vector.tensor_copy(out=bo_s[:], in_=bo_s_raw[:])
+            nc.vector.tensor_copy(out=bo_t[:], in_=bo_t_raw[:])
 
         log_det = const.tile([P, ROWS_PP], F32, name="log_det")
 
-        hq, hc, hsc, gt, gg, gc, gsc, o_ps = {}, {}, {}, {}, {}, {}, {}, {}
+        hq, hc, hsc, gt, gg, gc, gsc, os_ps, ot_ps = {}, {}, {}, {}, {}, {}, {}, {}, {}
         ls_t, ex_t, ot_t, sh_t, mz_t = {}, {}, {}, {}, {}
 
         def transpose_h(u, vector_half=None):
@@ -209,29 +217,54 @@ def tile_affinecouplinglayer_pa_t_kernel(
             )
 
         def quantise_g(c):
-            cw = ring2.tile([P, 2 * COLS], U32, name="gc", align_bytes=64)
-            sw = ring2.tile([P, 2 * COLS], U8, name="gsc", align_bytes=64)
+            cw = ring4.tile([P, 2 * COLS], U32, name="gc", align_bytes=64)
+            sw = ring4.tile([P, 2 * COLS], U8, name="gsc", align_bytes=64)
             nc.vector.quantize_mx(out=cw[:].bitcast(FP8X4), scales=sw[:], in_=gg[c][:].rearrange("p b t -> p (b t)"))
             gc[c], gsc[c] = cw, sw
 
-        def output_layer(c):
-            for n in range(2):
-                o = m2_pool.tile([P, TILES, D_OUT], F32, name="m2")
-                o_ps[(c, n)] = o
-                for r in range(TILES):
-                    cols = slice(n * COLS + r * P, n * COLS + (r + 1) * P)
-                    nc.tensor.matmul_mx(
-                        out=o[:, r, :],
-                        lhsT=gc[c][:, cols].bitcast(FP8X4),
-                        lhsT_scale=gsc[c][:, cols],
-                        rhs=woc[n][:].bitcast(FP8X4),
-                        rhs_scale=wosc[n][:],
-                        start=True,
-                        stop=True,
-                    )
+        def scale_output(c):
+            o = os_pool.tile([P, TILES, D_OUT], F32, name="os")
+            os_ps[c] = o
+            for r in range(TILES):
+                cols = slice(r * P, (r + 1) * P)
+                nc.tensor.matmul_mx(
+                    out=o[:, r, :],
+                    lhsT=gc[c][:, cols].bitcast(FP8X4),
+                    lhsT_scale=gsc[c][:, cols],
+                    rhs=woc[0][:].bitcast(FP8X4),
+                    rhs_scale=wosc[0][:],
+                    start=True,
+                    stop=True,
+                )
 
-        def bias_rows(n):
-            return bo[n][:].unsqueeze(1).to_broadcast([P, TILES, D_OUT])
+        def at_end(c):
+            return 2 * c + 6 >= N_UNITS
+
+        def shift_output(c):
+            if at_end(c):
+                o = m1_pool.tile([P, COLS], F32, name="m1")
+            else:
+                o = ot_pool.tile([P, COLS], F32, name="ot_ps")
+            ot_ps[c] = o
+            nc.tensor.matmul_mx(
+                out=o[:],
+                lhsT=woc[1][:].bitcast(FP8X4),
+                lhsT_scale=wosc[1][:],
+                rhs=gc[c][:, COLS : 2 * COLS].bitcast(FP8X4),
+                rhs_scale=gsc[c][:, COLS : 2 * COLS],
+                start=True,
+                stop=True,
+            )
+
+        def add_shift_bias(c):
+            sh = ring2.tile([P, COLS], F32, name="sh")
+            sh_t[c] = sh
+            nc.scalar.activation(out=sh[:], in_=ot_ps[c][:], func=ACT.Identity, bias=bo_t[:], scale=1.0)
+
+        def transpose_shift(c):
+            for r in range(TILES):
+                cols = slice(r * P, (r + 1) * P)
+                nc.tensor.transpose(ot_ps[c][:, cols], sh_t[c][:, cols], ident[:])
 
         def z_rows(c, lo):
             i0 = (c % 2) * TILES
@@ -240,12 +273,7 @@ def tile_affinecouplinglayer_pa_t_kernel(
         def add_scale_bias(c):
             ls = ring3.tile([P, TILES, D_OUT], F32, name="ls")
             ls_t[c] = ls
-            nc.vector.tensor_tensor(out=ls[:], in0=o_ps[(c, 0)][:], in1=bias_rows(0), op=ALU.add)
-
-        def add_shift_bias(c):
-            sh = ring3.tile([P, TILES, D_OUT], F32, name="sh")
-            sh_t[c] = sh
-            nc.vector.tensor_tensor(out=sh[:], in0=o_ps[(c, 1)][:], in1=bias_rows(1), op=ALU.add)
+            nc.vector.tensor_tensor(out=ls[:], in0=os_ps[c][:], in1=bo_s[:].unsqueeze(1).to_broadcast([P, TILES, D_OUT]), op=ALU.add)
 
         def clamp(c):
             ls = ls_t[c]
@@ -259,9 +287,13 @@ def tile_affinecouplinglayer_pa_t_kernel(
         def row_sums(c):
             nc.vector.tensor_reduce(out=log_det[:, c * TILES : (c + 1) * TILES], in_=ls_t[c][:], axis=AX.X, op=ALU.add)
 
-        def scale_z2(c):
+        def release_gpsimd(c):
             mz = gate.tile([P, TILES, D_OUT], F32, name="mz")
             mz_t[c] = mz
+            nc.vector.memset(mz[:, 0, 0:1], 0.0)
+
+        def scale_z2(c):
+            mz = mz_t[c]
             nc.gpsimd.tensor_tensor(out=mz[:], in0=z_rows(c, D_OUT), in1=ex_t[c][:], op=ALU.mult)
 
         def cast_z1(c):
@@ -277,13 +309,18 @@ def tile_affinecouplinglayer_pa_t_kernel(
             )
 
         def finish(c):
-            nc.vector.tensor_tensor(out=ot_t[c][:, :, D_OUT:DIM], in0=mz_t[c][:], in1=sh_t[c][:], op=ALU.add)
+            nc.vector.tensor_tensor(out=ot_t[c][:, :, D_OUT:DIM], in0=ot_ps[c][:].rearrange("p (r d) -> p r d", d=D_OUT), in1=mz_t[c][:], op=ALU.add)
             nc.sync.dma_start(out=z_out[:, c * TILES : (c + 1) * TILES, :], in_=ot_t[c][:])
 
         def when(it, first, fn):
             c = (it - first) // 2
             if it >= first and (it - first) % 2 == 0 and c < N_CHUNKS:
                 fn(c)
+
+        def when_shift(it, delay, fn):
+            for c in range(N_CHUNKS):
+                if it == 2 * c + (6 if at_end(c) else 8) + delay:
+                    fn(c)
 
         prep_w(0)
         transpose_h(0)
@@ -293,31 +330,36 @@ def tile_affinecouplinglayer_pa_t_kernel(
 
         for it in range(N_UNITS + 8):
             vector_copies = []
+            when_shift(it, 1, add_shift_bias)
             when(it, 7, exponential)
             if it < N_UNITS:
                 hidden_layer(it)
             if it == 0:
                 prep_wout(0)
                 prep_wout(1)
+                prep_bout()
                 transpose_h(2)
             if it + 3 < N_UNITS:
                 if (it + 3) % 4 == 0 and (it + 3) // 4 + 1 < N_LOADS:
                     load((it + 3) // 4 + 1)
-                vector_copies = transpose_h(it + 3, 1 if it % 4 == 1 else None)
-            when(it, 4, output_layer)
+                vector_copies = transpose_h(it + 3, 1 if it % 2 == 1 else None)
+            when_shift(it, 1, transpose_shift)
+            when(it, 4, scale_output)
+            when_shift(it, 0, shift_output)
             if it == 0:
                 quantise_h(0, 1, 2)
             if it % 2 == 1 and (it + 1) // 2 < N_CHUNKS:
                 quantise_h((it + 1) // 2, 0, 2)
-            when(it, 9, finish)
+            when(it, 7, release_gpsimd)
             when(it, 7, scale_z2)
             when(it, 7, cast_z1)
             when(it, 5, add_scale_bias)
-            when(it, 5, add_shift_bias)
             for dst, src in vector_copies:
                 nc.vector.tensor_copy(out=dst, in_=src)
             when(it, 7, row_sums)
+            when(it, 5, lambda c: clamp(c) if at_end(c) else None)
+            when_shift(it, 1, finish)
             when(it, 2, regroup_g)
-            when(it, 6, clamp)
+            when(it, 6, lambda c: None if at_end(c) else clamp(c))
             when(it, 2, quantise_g)
         nc.sync.dma_start(out=out_1.rearrange("(p i) -> p i", i=ROWS_PP), in_=log_det[:])

@@ -85,10 +85,11 @@ def tile_affinecouplinglayer_pa_t_kernel(
             wo = const.tile([P, HID], BF16, name="wo_sb%d" % n)
             nc.scalar.dma_start(out=wo[:], in_=w_out[n])
             wo_sb.append(wo)
-        bo_s_raw = const.tile([P, D_OUT], BF16, name="bo_s_raw")
-        nc.scalar.dma_start(out=bo_s_raw[:], in_=b_out[0].partition_broadcast(P))
-        bo_t_raw = const.tile([P, 1], BF16, name="bo_t_raw")
-        nc.scalar.dma_start(out=bo_t_raw[:], in_=b_out[1].rearrange("(p o) -> p o", o=1))
+        bo_raw = []
+        for n in range(2):
+            br = const.tile([P, 1], BF16, name="bo_raw%d" % n)
+            nc.scalar.dma_start(out=br[:], in_=b_out[n].rearrange("(p o) -> p o", o=1))
+            bo_raw.append(br)
         for n in range(2):
             load_h_rows(n, 0, TILES, LOAD_TILES)
         z0 = zpool.tile([P, LOAD_TILES, DIM], BF16, name="zt")
@@ -156,9 +157,14 @@ def tile_affinecouplinglayer_pa_t_kernel(
         bo_s = const.tile([P, D_OUT], F32, name="bo_s")
         bo_t = const.tile([P, 1], F32, name="bo_t")
 
+        bo_s_col = const.tile([P, 1], F32, name="bo_s_col")
+
         def prep_bout():
-            nc.vector.tensor_copy(out=bo_s[:], in_=bo_s_raw[:])
-            nc.vector.tensor_copy(out=bo_t[:], in_=bo_t_raw[:])
+            nc.vector.tensor_copy(out=bo_s_col[:], in_=bo_raw[0][:])
+            nc.vector.tensor_copy(out=bo_t[:], in_=bo_raw[1][:])
+            bank = os_pool.tile([P, 2, 2 * P], F32, name="os")
+            nc.tensor.matmul(bank[:, 0, 0:P], bo_s_col[:].to_broadcast([P, P]), ident[:], start=True, stop=True)
+            nc.vector.tensor_copy(out=bo_s[:], in_=bank[:, 0, 0:P])
 
         log_det = const.tile([P, ROWS_PP], F32, name="log_det")
 

@@ -99,6 +99,8 @@ def tile_affinecouplinglayer_pa_t_kernel(
 
         ident = const.tile([P, P], F32, name="ident")
         make_identity(nc, ident[:])
+        ones = const.tile([P, 1], F32, name="ones")
+        nc.gpsimd.memset(ones[:], 1.0)
 
         def to_k_major(words, first_word, grouped_words, weights, vector_half):
             later = []
@@ -143,6 +145,9 @@ def tile_affinecouplinglayer_pa_t_kernel(
             wv = wo_sb[n][:].bitcast(F32).rearrange("p (q u) -> p u q", u=2)
             for u in range(2):
                 nc.tensor.transpose(bank[:, u, 0:P], wv[:, u, :], ident[:])
+            if n == 0:
+                nc.tensor.matmul(bank[:, 0, P : 2 * P], bo_s_col[:].to_broadcast([P, P]), ident[:], start=True, stop=True)
+                nc.vector.tensor_copy(out=bo_s[:], in_=bank[:, 0, P : 2 * P])
             woq = const.tile([P, PACK * D_OUT], BF16, name="woq%d" % n, align_bytes=64)
             nc.vector.tensor_copy(
                 out=woq[:].bitcast(F32).rearrange("p (b u) -> p b u", u=2),
@@ -162,14 +167,11 @@ def tile_affinecouplinglayer_pa_t_kernel(
         def prep_bout():
             nc.vector.tensor_copy(out=bo_s_col[:], in_=bo_raw[0][:])
             nc.vector.tensor_copy(out=bo_t[:], in_=bo_raw[1][:])
-            bank = os_pool.tile([P, 2, 2 * P], F32, name="os")
-            nc.tensor.matmul(bank[:, 0, 0:P], bo_s_col[:].to_broadcast([P, P]), ident[:], start=True, stop=True)
-            nc.vector.tensor_copy(out=bo_s[:], in_=bank[:, 0, 0:P])
 
         log_det = const.tile([P, ROWS_PP], F32, name="log_det")
 
         hq, hc, hsc, gt, gg, gc, gsc, os_ps, ot_ps = {}, {}, {}, {}, {}, {}, {}, {}, {}
-        ls_t, ex_t, ot_t, sh_t, mz_t = {}, {}, {}, {}, {}
+        ls_t, ex_t, ot_t, sh_t, mz_t, o_t, rs_ps = {}, {}, {}, {}, {}, {}, {}
 
         def transpose_h(u, vector_half=None):
             c, n = u // 2, u % 2
@@ -197,10 +199,15 @@ def tile_affinecouplinglayer_pa_t_kernel(
 
         def hidden_layer(u):
             c, n = u // 2, u % 2
-            if n == 0:
-                g = ring3.tile([P, PACK, 2 * COLS], BF16, name="gt")
-                gt[c] = g
             cols = slice(n * COLS, (n + 1) * COLS)
+            if c == N_CHUNKS - 1:
+                g = ring3.tile([P, PACK, COLS], BF16, name="gt")
+                gt[(c, n)] = g[:]
+            else:
+                if n == 0:
+                    g = ring3.tile([P, PACK, 2 * COLS], BF16, name="gt")
+                    gt[c] = g
+                gt[(c, n)] = gt[c][:, :, cols]
             for t in range(PACK):
                 acc = m1_pool.tile([P, COLS], F32, name="m1")
                 nc.tensor.matmul_mx(
@@ -212,21 +219,30 @@ def tile_affinecouplinglayer_pa_t_kernel(
                     start=True,
                     stop=True,
                 )
-                nc.scalar.activation(out=gt[c][:, t, cols], in_=acc[:], func=ACT.Relu, bias=bh[n][:, t : t + 1], scale=1.0)
+                nc.scalar.activation(out=gt[(c, n)][:, t, :], in_=acc[:], func=ACT.Relu, bias=bh[n][:, t : t + 1], scale=1.0)
 
-        def regroup_g(c):
-            t = ring2.tile([P, 2 * COLS, PACK], BF16, name="gg", align_bytes=64)
-            gg[c] = t
+        def regroup_g(c, n0=0, n1=2):
+            if n0 == 0:
+                t = ring2.tile([P, 2 * COLS, PACK], BF16, name="gg", align_bytes=64)
+                gg[c] = t
+            cols = slice(n0 * COLS, n1 * COLS)
+            src = gt[c][:] if n1 - n0 == 2 else gt[(c, n0)]
             nc.vector.tensor_copy(
-                out=t[:].rearrange("p (c i) t -> p c t i", i=4),
-                in_=gt[c][:].rearrange("p t (c i) -> p c t i", i=4),
+                out=gg[c][:, cols, :].rearrange("p (c i) t -> p c t i", i=4),
+                in_=src.rearrange("p t (c i) -> p c t i", i=4),
             )
 
-        def quantise_g(c):
-            cw = ring4.tile([P, 2 * COLS], U32, name="gc", align_bytes=64)
-            sw = ring4.tile([P, 2 * COLS], U8, name="gsc", align_bytes=64)
-            nc.vector.quantize_mx(out=cw[:].bitcast(FP8X4), scales=sw[:], in_=gg[c][:].rearrange("p b t -> p (b t)"))
-            gc[c], gsc[c] = cw, sw
+        def quantise_g(c, n0=0, n1=2):
+            if n0 == 0:
+                cw = ring4.tile([P, 2 * COLS], U32, name="gc", align_bytes=64)
+                sw = ring4.tile([P, 2 * COLS], U8, name="gsc", align_bytes=64)
+                gc[c], gsc[c] = cw, sw
+            cols = slice(n0 * COLS, n1 * COLS)
+            nc.vector.quantize_mx(
+                out=gc[c][:, cols].bitcast(FP8X4),
+                scales=gsc[c][:, cols],
+                in_=gg[c][:, cols, :].rearrange("p b t -> p (b t)"),
+            )
 
         def scale_output(c):
             o = os_pool.tile([P, TILES, D_OUT], F32, name="os")
@@ -246,21 +262,61 @@ def tile_affinecouplinglayer_pa_t_kernel(
         def at_end(c):
             return 2 * c + 6 >= N_UNITS
 
-        def shift_output(c):
-            if at_end(c):
+        def spare_bank(pool):
+            if pool == "tp":
+                o = tp_pool.tile([P, COLS], F32, name="tp")
+            elif pool == "m1":
                 o = m1_pool.tile([P, COLS], F32, name="m1")
+            elif pool == "os":
+                o = os_pool.tile([P, COLS], F32, name="os")
             else:
                 o = ot_pool.tile([P, COLS], F32, name="ot_ps")
-            ot_ps[c] = o
+            return o
+
+        def output_t(n, c, pool):
+            o = spare_bank(pool)
+            o_t[(n, c)] = o
             nc.tensor.matmul_mx(
                 out=o[:],
-                lhsT=woc[1][:].bitcast(FP8X4),
-                lhsT_scale=wosc[1][:],
-                rhs=gc[c][:, COLS : 2 * COLS].bitcast(FP8X4),
-                rhs_scale=gsc[c][:, COLS : 2 * COLS],
+                lhsT=woc[n][:].bitcast(FP8X4),
+                lhsT_scale=wosc[n][:],
+                rhs=gc[c][:, n * COLS : (n + 1) * COLS].bitcast(FP8X4),
+                rhs_scale=gsc[c][:, n * COLS : (n + 1) * COLS],
                 start=True,
                 stop=True,
             )
+
+        def shift_output(c, pool="ot"):
+            output_t(1, c, pool)
+            ot_ps[c] = o_t[(1, c)]
+
+        def scale_output_t(c, pool):
+            output_t(0, c, pool)
+
+        def add_scale_bias_t(c):
+            ls = ring3.tile([P, TILES, D_OUT], F32, name="ls")
+            ls_t[c] = ls
+            nc.scalar.activation(
+                out=ls[:].rearrange("p r d -> p (r d)"), in_=o_t[(0, c)][:], func=ACT.Identity, bias=bo_s_col[:], scale=1.0
+            )
+
+        def transpose_scale(c):
+            for r in range(TILES):
+                nc.tensor.transpose(o_t[(0, c)][:, r * P : (r + 1) * P], ls_t[c][:, r, :], ident[:])
+
+        def row_sums_t(c, pool):
+            o = spare_bank(pool)
+            for r in range(TILES):
+                nc.tensor.matmul(o[:, r : r + 1], ls_t[c][:, r, :], ones[:], start=True, stop=True)
+            rs_ps[c] = o
+
+        def copy_row_sums(c):
+            nc.vector.tensor_copy(out=log_det[:, c * TILES : (c + 1) * TILES], in_=rs_ps[c][:, 0:TILES])
+
+        def log_s_rows(c):
+            if (0, c) in o_t:
+                return o_t[(0, c)][:].rearrange("p (r d) -> p r d", d=D_OUT)
+            return ls_t[c][:]
 
         def add_shift_bias(c):
             sh = ring2.tile([P, COLS], F32, name="sh")
@@ -288,23 +344,29 @@ def tile_affinecouplinglayer_pa_t_kernel(
         def exponential(c):
             ex = ring2.tile([P, TILES, D_OUT], F32, name="ex")
             ex_t[c] = ex
-            nc.scalar.activation(out=ex[:], in_=ls_t[c][:], func=ACT.Exp)
+            nc.scalar.activation(out=ex[:], in_=log_s_rows(c), func=ACT.Exp)
 
         def row_sums(c):
-            nc.vector.tensor_reduce(out=log_det[:, c * TILES : (c + 1) * TILES], in_=ls_t[c][:], axis=AX.X, op=ALU.add)
+            nc.vector.tensor_reduce(out=log_det[:, c * TILES : (c + 1) * TILES], in_=log_s_rows(c), axis=AX.X, op=ALU.add)
 
         def release_gpsimd(c):
             mz = gate.tile([P, TILES, D_OUT], F32, name="mz")
             mz_t[c] = mz
             nc.vector.memset(mz[:, 0, 0:1], 0.0)
 
-        def scale_z2(c):
+        def scale_z2(c, engine=nc.gpsimd):
+            if c not in mz_t:
+                mz = gate.tile([P, TILES, D_OUT], F32, name="mz")
+                mz_t[c] = mz
             mz = mz_t[c]
-            nc.gpsimd.tensor_tensor(out=mz[:], in0=z_rows(c, D_OUT), in1=ex_t[c][:], op=ALU.mult)
+            engine.tensor_tensor(out=mz[:], in0=z_rows(c, D_OUT), in1=ex_t[c][:], op=ALU.mult)
 
-        def cast_z1(c):
+        def cast_z1(c, engine=nc.gpsimd):
             ot = ring4.tile([P, TILES, DIM], F32, name="ot")
             ot_t[c] = ot
+            if engine is nc.scalar:
+                nc.scalar.copy(out=ot[:, :, 0:D_OUT], in_=z_rows(c, 0))
+                return
             nc.gpsimd.tensor_scalar(
                 out=ot[:, :, 0:D_OUT],
                 in0=z_rows(c, 0),
@@ -332,9 +394,10 @@ def tile_affinecouplinglayer_pa_t_kernel(
         transpose_h(0)
         quantise_h(0, 0, 1)
         prep_w(1)
+        prep_bout()
         transpose_h(1)
 
-        for it in range(N_UNITS + 8):
+        for it in range(N_UNITS):
             vector_copies = []
             when_shift(it, 1, add_shift_bias)
             when(it, 7, exponential)
@@ -343,14 +406,13 @@ def tile_affinecouplinglayer_pa_t_kernel(
             if it == 0:
                 prep_wout(0)
                 prep_wout(1)
-                prep_bout()
                 transpose_h(2)
             if it + 3 < N_UNITS:
                 if (it + 3) % 4 == 0 and (it + 3) // 4 + 1 < N_LOADS:
                     load((it + 3) // 4 + 1)
                 vector_copies = transpose_h(it + 3, 1 if it % 2 == 1 else None)
             when_shift(it, 1, transpose_shift)
-            when(it, 4, scale_output)
+            when(it, 4, lambda c: None if at_end(c) else scale_output(c))
             when_shift(it, 0, shift_output)
             if it == 0:
                 quantise_h(0, 1, 2)
@@ -359,13 +421,56 @@ def tile_affinecouplinglayer_pa_t_kernel(
             when(it, 7, release_gpsimd)
             when(it, 7, scale_z2)
             when(it, 7, cast_z1)
-            when(it, 5, add_scale_bias)
+            when(it, 5, lambda c: None if at_end(c) else add_scale_bias(c))
             for dst, src in vector_copies:
                 nc.vector.tensor_copy(out=dst, in_=src)
             when(it, 7, row_sums)
-            when(it, 5, lambda c: clamp(c) if at_end(c) else None)
             when_shift(it, 1, finish)
             when(it, 2, regroup_g)
             when(it, 6, lambda c: None if at_end(c) else clamp(c))
             when(it, 2, quantise_g)
+        scale_output_t(13, "tp")
+        scale_output_t(14, "os")
+        shift_output(12)
+        shift_output(13, "tp")
+        shift_output(14, "m1")
+        regroup_g(15, 0, 1)
+        add_scale_bias_t(13)
+        add_scale_bias_t(14)
+        add_shift_bias(12)
+        add_shift_bias(13)
+        regroup_g(15, 1, 2)
+        clamp(13)
+        clamp(14)
+        quantise_g(15)
+        transpose_scale(13)
+        transpose_shift(12)
+        transpose_scale(14)
+        transpose_shift(13)
+        exponential(13)
+        exponential(14)
+        scale_output_t(15, "m1")
+        shift_output(15, "m1")
+        add_shift_bias(14)
+        add_scale_bias_t(15)
+        cast_z1(13, nc.scalar)
+        transpose_shift(14)
+        finish(12)
+        scale_z2(13, nc.vector)
+        scale_z2(14, nc.vector)
+        clamp(15)
+        transpose_scale(15)
+        finish(13)
+        add_shift_bias(15)
+        exponential(15)
+        transpose_shift(15)
+        cast_z1(14, nc.scalar)
+        row_sums_t(13, "m1")
+        cast_z1(15, nc.scalar)
+        finish(14)
+        scale_z2(15, nc.vector)
+        row_sums(14)
+        finish(15)
+        row_sums(15)
+        copy_row_sums(13)
         nc.sync.dma_start(out=out_1.rearrange("(p i) -> p i", i=ROWS_PP), in_=log_det[:])

@@ -73,25 +73,36 @@ def tile_affinecouplinglayer_pa_t_kernel(
             z_sb[s] = t
             nc.sync.dma_start(out=t[:], in_=z_in[:, s * LOAD_TILES : (s + 1) * LOAD_TILES, :])
 
+        def load_w(n, t0, t1):
+            nc.sync.dma_start(
+                out=w_sb[n][:, t0 * HID : t1 * HID].rearrange("p (t k) -> p t k", k=HID),
+                in_=w_hid[n].rearrange("(p t) k -> p t k", t=PACK)[:, t0:t1, :],
+            )
+
+        bo_raw = []
         for n in range(2):
-            wt = const.tile([P, PACK * HID], BF16, name="w_sb%d" % n)
-            nc.sync.dma_start(out=wt[:], in_=w_hid[n].rearrange("(p t) k -> p (t k)", t=PACK))
-            w_sb.append(wt)
-            new_h(n, 0)
-            load_h_rows(n, 0, 0, TILES)
             br = const.tile([P, PACK], BF16, name="bh_raw%d" % n)
             nc.scalar.dma_start(out=br[:], in_=b_hid[n].rearrange("(p t) -> p t", t=PACK))
             bh_raw.append(br)
-            wo = const.tile([P, HID], BF16, name="wo_sb%d" % n)
-            nc.scalar.dma_start(out=wo[:], in_=w_out[n])
-            wo_sb.append(wo)
-        bo_raw = []
         for n in range(2):
             br = const.tile([P, 1], BF16, name="bo_raw%d" % n)
             nc.scalar.dma_start(out=br[:], in_=b_out[n].rearrange("(p o) -> p o", o=1))
             bo_raw.append(br)
         for n in range(2):
+            wt = const.tile([P, PACK * HID], BF16, name="w_sb%d" % n)
+            w_sb.append(wt)
+            new_h(n, 0)
+        load_w(0, 0, 2)
+        load_w(0, 2, PACK)
+        load_h_rows(0, 0, 0, TILES)
+        load_h_rows(1, 0, 0, TILES)
+        load_w(1, 0, PACK)
+        for n in range(2):
             load_h_rows(n, 0, TILES, LOAD_TILES)
+        for n in range(2):
+            wo = const.tile([P, HID], BF16, name="wo_sb%d" % n)
+            nc.sync.dma_start(out=wo[:], in_=w_out[n])
+            wo_sb.append(wo)
         z0 = zpool.tile([P, LOAD_TILES, DIM], BF16, name="zt")
         z_sb[0] = z0
         nc.sync.dma_start(out=z0[:], in_=z_in[:, 0:LOAD_TILES, :])
@@ -99,14 +110,16 @@ def tile_affinecouplinglayer_pa_t_kernel(
 
         ident = const.tile([P, P], F32, name="ident")
         make_identity(nc, ident[:])
-        ones = const.tile([P, 1], F32, name="ones")
-        nc.gpsimd.memset(ones[:], 1.0)
 
-        def to_k_major(words, first_word, grouped_words, weights, vector_half):
+        def to_k_major(words, first_word, grouped_words, weights, vector_halves):
             later = []
             for half in range(2):
-                if weights:
+                if weights == 1:
                     bank = m1_pool.tile([P, 2, 2 * P], F32, name="m1")
+                elif weights and half == 0:
+                    bank = os_pool.tile([P, 2, 2 * P], F32, name="os")
+                elif weights:
+                    bank = ot_pool.tile([P, 2, 2 * P], F32, name="ot_ps")
                 else:
                     bank = tp_pool.tile([P, 2, 2 * P], F32, name="tp")
                 for r in range(2):
@@ -117,22 +130,29 @@ def tile_affinecouplinglayer_pa_t_kernel(
                 src = bank[:].rearrange("p u b -> p b u")
                 if weights:
                     nc.vector.tensor_copy(out=dst, in_=src)
-                elif half == vector_half:
+                elif half in vector_halves:
                     later.append((dst, src))
                 else:
                     nc.scalar.copy(out=dst, in_=src)
             return later
 
         wc, wsc, woc, wosc, bh = [], [], [], [], []
+        wq_t = {}
 
-        def prep_w(n):
+        def transpose_w(n):
             wq = const.tile([P, PACK * HID], BF16, name="wq%d" % n, align_bytes=64)
-            to_k_major(w_sb[n][:].bitcast(F32), 0, wq[:].bitcast(F32), True, None)
+            wq_t[n] = wq
+            to_k_major(w_sb[n][:].bitcast(F32), 0, wq[:].bitcast(F32), n + 1, ())
+
+        def quantise_w(n):
+            wq = wq_t[n]
             c = const.tile([P, HID], U32, name="wc%d" % n, align_bytes=64)
             s = const.tile([P, HID], U8, name="wsc%d" % n, align_bytes=64)
             nc.vector.quantize_mx(out=c[:].bitcast(FP8X4), scales=s[:], in_=wq[:])
             wc.append(c)
             wsc.append(s)
+
+        def prep_bias(n):
             b32 = const.tile([P, PACK], F32, name="bh%d" % n)
             nc.vector.tensor_copy(out=b32[:], in_=bh_raw[n][:])
             bh.append(b32)
@@ -171,9 +191,9 @@ def tile_affinecouplinglayer_pa_t_kernel(
         log_det = const.tile([P, ROWS_PP], F32, name="log_det")
 
         hq, hc, hsc, gt, gg, gc, gsc, os_ps, ot_ps = {}, {}, {}, {}, {}, {}, {}, {}, {}
-        ls_t, ex_t, ot_t, sh_t, mz_t, o_t, rs_ps = {}, {}, {}, {}, {}, {}, {}
+        ls_t, ex_t, ot_t, sh_t, mz_t, o_t = {}, {}, {}, {}, {}, {}
 
-        def transpose_h(u, vector_half=None):
+        def transpose_h(u, vector_halves=()):
             c, n = u // 2, u % 2
             if n == 0:
                 t = ring3.tile([P, 2 * PACK * COLS], BF16, name="hq", align_bytes=64)
@@ -183,7 +203,7 @@ def tile_affinecouplinglayer_pa_t_kernel(
                 (c % 2) * TILES * WORDS,
                 hq[c][:].bitcast(F32)[:, n * 2 * COLS : (n + 1) * 2 * COLS],
                 False,
-                vector_half,
+                vector_halves,
             )
 
         def quantise_h(c, n0, n1):
@@ -304,15 +324,6 @@ def tile_affinecouplinglayer_pa_t_kernel(
             for r in range(TILES):
                 nc.tensor.transpose(o_t[(0, c)][:, r * P : (r + 1) * P], ls_t[c][:, r, :], ident[:])
 
-        def row_sums_t(c, pool):
-            o = spare_bank(pool)
-            for r in range(TILES):
-                nc.tensor.matmul(o[:, r : r + 1], ls_t[c][:, r, :], ones[:], start=True, stop=True)
-            rs_ps[c] = o
-
-        def copy_row_sums(c):
-            nc.vector.tensor_copy(out=log_det[:, c * TILES : (c + 1) * TILES], in_=rs_ps[c][:, 0:TILES])
-
         def log_s_rows(c):
             if (0, c) in o_t:
                 return o_t[(0, c)][:].rearrange("p (r d) -> p r d", d=D_OUT)
@@ -390,40 +401,54 @@ def tile_affinecouplinglayer_pa_t_kernel(
                 if it == 2 * c + (6 if at_end(c) else 8) + delay:
                     fn(c)
 
-        prep_w(0)
-        transpose_h(0)
-        quantise_h(0, 0, 1)
-        prep_w(1)
-        prep_bout()
-        transpose_h(1)
+        def copy_on_vector(copies):
+            for dst, src in copies:
+                nc.vector.tensor_copy(out=dst, in_=src)
 
-        for it in range(N_UNITS):
+        transpose_w(0)
+        prep_bias(0)
+        transpose_h(0)
+        quantise_w(0)
+        quantise_h(0, 0, 1)
+        transpose_h(1)
+        prep_bias(1)
+        transpose_w(1)
+        hidden_layer(0)
+        quantise_h(0, 1, 2)
+        copies = transpose_h(2, (0, 1))
+        quantise_w(1)
+        prep_bout()
+        copy_on_vector(copies)
+        hidden_layer(1)
+        copies = transpose_h(3, (1,))
+        quantise_h(1, 0, 1)
+        copy_on_vector(copies)
+        prep_wout(0)
+        quantise_h(1, 1, 2)
+        load(2)
+        transpose_h(4)
+        prep_wout(1)
+
+        for it in range(2, N_UNITS):
             vector_copies = []
             when_shift(it, 1, add_shift_bias)
             when(it, 7, exponential)
             if it < N_UNITS:
                 hidden_layer(it)
-            if it == 0:
-                prep_wout(0)
-                prep_wout(1)
-                transpose_h(2)
             if it + 3 < N_UNITS:
                 if (it + 3) % 4 == 0 and (it + 3) // 4 + 1 < N_LOADS:
                     load((it + 3) // 4 + 1)
-                vector_copies = transpose_h(it + 3, 1 if it % 2 == 1 else None)
+                vector_copies = transpose_h(it + 3, (1,) if it % 2 == 1 else ())
             when_shift(it, 1, transpose_shift)
             when(it, 4, lambda c: None if at_end(c) else scale_output(c))
             when_shift(it, 0, shift_output)
-            if it == 0:
-                quantise_h(0, 1, 2)
             if it % 2 == 1 and (it + 1) // 2 < N_CHUNKS:
                 quantise_h((it + 1) // 2, 0, 2)
             when(it, 7, release_gpsimd)
             when(it, 7, scale_z2)
             when(it, 7, cast_z1)
             when(it, 5, lambda c: None if at_end(c) else add_scale_bias(c))
-            for dst, src in vector_copies:
-                nc.vector.tensor_copy(out=dst, in_=src)
+            copy_on_vector(vector_copies)
             when(it, 7, row_sums)
             when_shift(it, 1, finish)
             when(it, 2, regroup_g)
@@ -455,22 +480,23 @@ def tile_affinecouplinglayer_pa_t_kernel(
         add_scale_bias_t(15)
         cast_z1(13, nc.scalar)
         transpose_shift(14)
+        release_gpsimd(13)
+        scale_z2(13)
         finish(12)
-        scale_z2(13, nc.vector)
-        scale_z2(14, nc.vector)
+        row_sums(14)
         clamp(15)
         transpose_scale(15)
+        release_gpsimd(14)
+        scale_z2(14)
         finish(13)
+        row_sums(13)
         add_shift_bias(15)
         exponential(15)
         transpose_shift(15)
         cast_z1(14, nc.scalar)
-        row_sums_t(13, "m1")
         cast_z1(15, nc.scalar)
-        finish(14)
         scale_z2(15, nc.vector)
-        row_sums(14)
-        finish(15)
+        finish(14)
         row_sums(15)
-        copy_row_sums(13)
+        finish(15)
         nc.sync.dma_start(out=out_1.rearrange("(p i) -> p i", i=ROWS_PP), in_=log_det[:])

@@ -248,8 +248,8 @@ def tile_affinecouplinglayer_pa_t_kernel(
             cols = slice(n0 * COLS, n1 * COLS)
             src = gt[c][:] if n1 - n0 == 2 else gt[(c, n0)]
             nc.vector.tensor_copy(
-                out=gg[c][:, cols, :].rearrange("p (c i) t -> p c t i", i=4),
-                in_=src.rearrange("p t (c i) -> p c t i", i=4),
+                out=gg[c][:, cols, :].rearrange("p (c i) t -> p c t i", i=8),
+                in_=src.rearrange("p t (c i) -> p c t i", i=8),
             )
 
         def quantise_g(c, n0=0, n1=2):

from contextlib import ExitStack

import concourse.mybir as mybir
from concourse.masks import make_identity

F32 = mybir.dt.float32
BF16 = mybir.dt.bfloat16
U32 = mybir.dt.uint32
U8 = mybir.dt.uint8
FP8X4 = mybir.dt.float8_e4m3fn_x4
ACT = mybir.ActivationFunctionType
ALU = mybir.AluOpType
AX = mybir.AxisListType

P = 128
B, DIM, HID, D_OUT = 8192, 256, 512, 128
PACK = 4
ROWS_PP = B // P
TILES = 4
COLS = TILES * P
LOAD_TILES = 8
N_CHUNKS = ROWS_PP // TILES
N_UNITS = 2 * N_CHUNKS
N_LOADS = ROWS_PP // LOAD_TILES
WORDS = HID // 2
FLOPS = 2 * 2 * B * HID * (HID + D_OUT)


def tile_affinecouplinglayer_pa_t_kernel(
    tc, z, h_s, h_t, s_Whid1, s_bhid1, s_Wout, s_bout, t_Whid1, t_bhid1, t_Wout, t_bout, out_0, out_1
):
    nc = tc.nc
    h_in = (h_s.rearrange("(p i) k -> p i k", i=ROWS_PP), h_t.rearrange("(p i) k -> p i k", i=ROWS_PP))
    z_in = z.rearrange("(p i) d -> p i d", i=ROWS_PP)
    z_out = out_0.rearrange("(p i) d -> p i d", i=ROWS_PP)
    w_hid = (s_Whid1, t_Whid1)
    b_hid = (s_bhid1, t_bhid1)
    w_out = (s_Wout, t_Wout)
    b_out = (s_bout, t_bout)

    with ExitStack() as ctx:
        const = ctx.enter_context(tc.tile_pool(name="const", bufs=1))
        hpool = ctx.enter_context(tc.tile_pool(name="hpool", bufs=3))
        zpool = ctx.enter_context(tc.tile_pool(name="zpool", bufs=5))
        ring2 = ctx.enter_context(tc.tile_pool(name="ring2", bufs=2))
        ring3 = ctx.enter_context(tc.tile_pool(name="ring3", bufs=3))
        ring4 = ctx.enter_context(tc.tile_pool(name="ring4", bufs=4))
        gate = ctx.enter_context(tc.tile_pool(name="gate", bufs=2))
        tp_pool = ctx.enter_context(tc.psum_pool(name="tp_pool", bufs=2))
        m1_pool = ctx.enter_context(tc.psum_pool(name="m1_pool", bufs=4))
        os_pool = ctx.enter_context(tc.psum_pool(name="os_pool", bufs=1))
        ot_pool = ctx.enter_context(tc.psum_pool(name="ot_pool", bufs=1))
        ctx.enter_context(tc.manual_schedule())

        h_sb, z_sb = {}, {}
        w_sb, wo_sb, bh_raw = [], [], []

        def load_h_rows(n, s, i0, i1):
            nc.sync.dma_start(
                out=h_sb[(n, s)][:, i0 * HID : i1 * HID].rearrange("p (i k) -> p i k", k=HID),
                in_=h_in[n][:, s * LOAD_TILES + i0 : s * LOAD_TILES + i1, :],
            )

        def new_h(n, s):
            t = hpool.tile([P, LOAD_TILES * HID], BF16, name="h%d" % n)
            h_sb[(n, s)] = t

        def load(s):
            for n in range(2):
                new_h(n, s)
                load_h_rows(n, s, 0, LOAD_TILES)
            t = zpool.tile([P, LOAD_TILES, DIM], BF16, name="zt")
            z_sb[s] = t
            nc.sync.dma_start(out=t[:], in_=z_in[:, s * LOAD_TILES : (s + 1) * LOAD_TILES, :])

        def load_w(n, t0, t1):
            nc.sync.dma_start(
                out=w_sb[n][:, t0 * HID : t1 * HID].rearrange("p (t k) -> p t k", k=HID),
                in_=w_hid[n].rearrange("(p t) k -> p t k", t=PACK)[:, t0:t1, :],
            )

        bo_raw = []
        for n in range(2):
            br = const.tile([P, PACK], BF16, name="bh_raw%d" % n)
            nc.scalar.dma_start(out=br[:], in_=b_hid[n].rearrange("(p t) -> p t", t=PACK))
            bh_raw.append(br)
        for n in range(2):
            br = const.tile([P, 1], BF16, name="bo_raw%d" % n)
            nc.scalar.dma_start(out=br[:], in_=b_out[n].rearrange("(p o) -> p o", o=1))
            bo_raw.append(br)
        for n in range(2):
            wt = const.tile([P, PACK * HID], BF16, name="w_sb%d" % n)
            w_sb.append(wt)
            new_h(n, 0)
        load_w(0, 0, 2)
        load_w(0, 2, PACK)
        load_h_rows(0, 0, 0, TILES)
        load_h_rows(1, 0, 0, TILES)
        load_w(1, 0, PACK)
        for n in range(2):
            load_h_rows(n, 0, TILES, LOAD_TILES)
        for n in range(2):
            wo = const.tile([P, HID], BF16, name="wo_sb%d" % n)
            nc.sync.dma_start(out=wo[:], in_=w_out[n])
            wo_sb.append(wo)
        z0 = zpool.tile([P, LOAD_TILES, DIM], BF16, name="zt")
        z_sb[0] = z0
        nc.sync.dma_start(out=z0[:], in_=z_in[:, 0:LOAD_TILES, :])
        load(1)

        ident = const.tile([P, P], F32, name="ident")
        make_identity(nc, ident[:])

        def to_k_major(words, first_word, grouped_words, weights, vector_halves):
            later = []
            for half in range(2):
                if weights == 1:
                    bank = m1_pool.tile([P, 2, 2 * P], F32, name="m1")
                elif weights and half == 0:
                    bank = os_pool.tile([P, 2, 2 * P], F32, name="os")
                elif weights:
                    bank = ot_pool.tile([P, 2, 2 * P], F32, name="ot_ps")
                else:
                    bank = tp_pool.tile([P, 2, 2 * P], F32, name="tp")
                for r in range(2):
                    for u in range(2):
                        w0 = first_word + (2 * half + r) * WORDS
                        nc.tensor.transpose(bank[:, u, r * P : (r + 1) * P], words[:, w0 + u : w0 + WORDS : 2], ident[:])
                dst = grouped_words[:, half * 4 * P : (half + 1) * 4 * P].rearrange("p (b u) -> p b u", u=2)
                src = bank[:].rearrange("p u b -> p b u")
                if weights:
                    nc.vector.tensor_copy(out=dst, in_=src)
                elif half in vector_halves:
                    later.append((dst, src))
                else:
                    nc.scalar.copy(out=dst, in_=src)
            return later

        wc, wsc, woc, wosc, bh = [], [], [], [], []
        wq_t = {}

        def transpose_w(n):
            wq = const.tile([P, PACK * HID], BF16, name="wq%d" % n, align_bytes=64)
            wq_t[n] = wq
            to_k_major(w_sb[n][:].bitcast(F32), 0, wq[:].bitcast(F32), n + 1, ())

        def quantise_w(n):
            wq = wq_t[n]
            c = const.tile([P, HID], U32, name="wc%d" % n, align_bytes=64)
            s = const.tile([P, HID], U8, name="wsc%d" % n, align_bytes=64)
            nc.vector.quantize_mx(out=c[:].bitcast(FP8X4), scales=s[:], in_=wq[:])
            wc.append(c)
            wsc.append(s)

        def prep_bias(n):
            b32 = const.tile([P, PACK], F32, name="bh%d" % n)
            nc.vector.tensor_copy(out=b32[:], in_=bh_raw[n][:])
            bh.append(b32)

        def prep_wout(n):
            if n == 0:
                bank = os_pool.tile([P, 2, 2 * P], F32, name="os")
            else:
                bank = ot_pool.tile([P, 2, 2 * P], F32, name="ot_ps")
            wv = wo_sb[n][:].bitcast(F32).rearrange("p (q u) -> p u q", u=2)
            for u in range(2):
                nc.tensor.transpose(bank[:, u, 0:P], wv[:, u, :], ident[:])
            if n == 0:
                nc.tensor.matmul(bank[:, 0, P : 2 * P], bo_s_col[:].to_broadcast([P, P]), ident[:], start=True, stop=True)
                nc.vector.tensor_copy(out=bo_s[:], in_=bank[:, 0, P : 2 * P])
            woq = const.tile([P, PACK * D_OUT], BF16, name="woq%d" % n, align_bytes=64)
            nc.vector.tensor_copy(
                out=woq[:].bitcast(F32).rearrange("p (b u) -> p b u", u=2),
                in_=bank[:, :, 0:P].rearrange("p u b -> p b u"),
            )
            c = const.tile([P, D_OUT], U32, name="woc%d" % n, align_bytes=64)
            s = const.tile([P, D_OUT], U8, name="wosc%d" % n, align_bytes=64)
            nc.vector.quantize_mx(out=c[:].bitcast(FP8X4), scales=s[:], in_=woq[:])
            woc.append(c)
            wosc.append(s)

        bo_s = const.tile([P, D_OUT], F32, name="bo_s")
        bo_t = const.tile([P, 1], F32, name="bo_t")

        bo_s_col = const.tile([P, 1], F32, name="bo_s_col")

        def prep_bout():
            nc.vector.tensor_copy(out=bo_s_col[:], in_=bo_raw[0][:])
            nc.vector.tensor_copy(out=bo_t[:], in_=bo_raw[1][:])

        log_det = const.tile([P, ROWS_PP], F32, name="log_det")

        hq, hc, hsc, gt, gg, gc, gsc, os_ps, ot_ps = {}, {}, {}, {}, {}, {}, {}, {}, {}
        ls_t, ex_t, ot_t, sh_t, mz_t, o_t = {}, {}, {}, {}, {}, {}

        def transpose_h(u, vector_halves=()):
            c, n = u // 2, u % 2
            if n == 0:
                t = ring3.tile([P, 2 * PACK * COLS], BF16, name="hq", align_bytes=64)
                hq[c] = t
            return to_k_major(
                h_sb[(n, c // 2)][:].bitcast(F32),
                (c % 2) * TILES * WORDS,
                hq[c][:].bitcast(F32)[:, n * 2 * COLS : (n + 1) * 2 * COLS],
                False,
                vector_halves,
            )

        def quantise_h(c, n0, n1):
            if n0 == 0:
                cw = ring3.tile([P, 2 * COLS], U32, name="hc", align_bytes=64)
                sw = ring3.tile([P, 2 * COLS], U8, name="hsc", align_bytes=64)
                hc[c], hsc[c] = cw, sw
            nc.vector.quantize_mx(
                out=hc[c][:, n0 * COLS : n1 * COLS].bitcast(FP8X4),
                scales=hsc[c][:, n0 * COLS : n1 * COLS],
                in_=hq[c][:, n0 * PACK * COLS : n1 * PACK * COLS],
            )

        def hidden_layer(u):
            c, n = u // 2, u % 2
            cols = slice(n * COLS, (n + 1) * COLS)
            if c == N_CHUNKS - 1:
                g = ring3.tile([P, PACK, COLS], BF16, name="gt")
                gt[(c, n)] = g[:]
            else:
                if n == 0:
                    g = ring3.tile([P, PACK, 2 * COLS], BF16, name="gt")
                    gt[c] = g
                gt[(c, n)] = gt[c][:, :, cols]
            for t in range(PACK):
                acc = m1_pool.tile([P, COLS], F32, name="m1")
                nc.tensor.matmul_mx(
                    out=acc[:],
                    lhsT=wc[n][:, t * P : (t + 1) * P].bitcast(FP8X4),
                    lhsT_scale=wsc[n][:, t * P : (t + 1) * P],
                    rhs=hc[c][:, cols].bitcast(FP8X4),
                    rhs_scale=hsc[c][:, cols],
                    start=True,
                    stop=True,
                )
                nc.scalar.activation(out=gt[(c, n)][:, t, :], in_=acc[:], func=ACT.Relu, bias=bh[n][:, t : t + 1], scale=1.0)

        def regroup_g(c, n0=0, n1=2):
            if n0 == 0:
                t = ring2.tile([P, 2 * COLS, PACK], BF16, name="gg", align_bytes=64)
                gg[c] = t
            cols = slice(n0 * COLS, n1 * COLS)
            src = gt[c][:] if n1 - n0 == 2 else gt[(c, n0)]
            nc.vector.tensor_copy(
                out=gg[c][:, cols, :].rearrange("p (c i) t -> p c t i", i=8),
                in_=src.rearrange("p t (c i) -> p c t i", i=8),
            )

        def quantise_g(c, n0=0, n1=2):
            if n0 == 0:
                cw = ring4.tile([P, 2 * COLS], U32, name="gc", align_bytes=64)
                sw = ring4.tile([P, 2 * COLS], U8, name="gsc", align_bytes=64)
                gc[c], gsc[c] = cw, sw
            cols = slice(n0 * COLS, n1 * COLS)
            nc.vector.quantize_mx(
                out=gc[c][:, cols].bitcast(FP8X4),
                scales=gsc[c][:, cols],
                in_=gg[c][:, cols, :].rearrange("p b t -> p (b t)"),
            )

        def scale_output(c):
            o = os_pool.tile([P, TILES, D_OUT], F32, name="os")
            os_ps[c] = o
            for r in range(TILES):
                cols = slice(r * P, (r + 1) * P)
                nc.tensor.matmul_mx(
                    out=o[:, r, :],
                    lhsT=gc[c][:, cols].bitcast(FP8X4),
                    lhsT_scale=gsc[c][:, cols],
                    rhs=woc[0][:].bitcast(FP8X4),
                    rhs_scale=wosc[0][:],
                    start=True,
                    stop=True,
                )

        def at_end(c):
            return 2 * c + 6 >= N_UNITS

        def spare_bank(pool):
            if pool == "tp":
                o = tp_pool.tile([P, COLS], F32, name="tp")
            elif pool == "m1":
                o = m1_pool.tile([P, COLS], F32, name="m1")
            elif pool == "os":
                o = os_pool.tile([P, COLS], F32, name="os")
            else:
                o = ot_pool.tile([P, COLS], F32, name="ot_ps")
            return o

        def output_t(n, c, pool):
            o = spare_bank(pool)
            o_t[(n, c)] = o
            nc.tensor.matmul_mx(
                out=o[:],
                lhsT=woc[n][:].bitcast(FP8X4),
                lhsT_scale=wosc[n][:],
                rhs=gc[c][:, n * COLS : (n + 1) * COLS].bitcast(FP8X4),
                rhs_scale=gsc[c][:, n * COLS : (n + 1) * COLS],
                start=True,
                stop=True,
            )

        def shift_output(c, pool="ot"):
            output_t(1, c, pool)
            ot_ps[c] = o_t[(1, c)]

        def scale_output_t(c, pool):
            output_t(0, c, pool)

        def add_scale_bias_t(c):
            ls = ring3.tile([P, TILES, D_OUT], F32, name="ls")
            ls_t[c] = ls
            nc.scalar.activation(
                out=ls[:].rearrange("p r d -> p (r d)"), in_=o_t[(0, c)][:], func=ACT.Identity, bias=bo_s_col[:], scale=1.0
            )

        def transpose_scale(c):
            for r in range(TILES):
                nc.tensor.transpose(o_t[(0, c)][:, r * P : (r + 1) * P], ls_t[c][:, r, :], ident[:])

        def log_s_rows(c):
            if (0, c) in o_t:
                return o_t[(0, c)][:].rearrange("p (r d) -> p r d", d=D_OUT)
            return ls_t[c][:]

        def add_shift_bias(c):
            sh = ring2.tile([P, COLS], F32, name="sh")
            sh_t[c] = sh
            nc.scalar.activation(out=sh[:], in_=ot_ps[c][:], func=ACT.Identity, bias=bo_t[:], scale=1.0)

        def transpose_shift(c):
            for r in range(TILES):
                cols = slice(r * P, (r + 1) * P)
                nc.tensor.transpose(ot_ps[c][:, cols], sh_t[c][:, cols], ident[:])

        def z_rows(c, lo):
            i0 = (c % 2) * TILES
            return z_sb[c // 2][:, i0 : i0 + TILES, lo : lo + D_OUT]

        def add_scale_bias(c):
            ls = ring3.tile([P, TILES, D_OUT], F32, name="ls")
            ls_t[c] = ls
            nc.vector.tensor_tensor(out=ls[:], in0=os_ps[c][:], in1=bo_s[:].unsqueeze(1).to_broadcast([P, TILES, D_OUT]), op=ALU.add)

        def clamp(c):
            ls = ls_t[c]
            nc.vector.tensor_scalar(out=ls[:], in0=ls[:], scalar1=-2.0, scalar2=2.0, op0=ALU.max, op1=ALU.min)

        def exponential(c):
            ex = ring2.tile([P, TILES, D_OUT], F32, name="ex")
            ex_t[c] = ex
            nc.scalar.activation(out=ex[:], in_=log_s_rows(c), func=ACT.Exp)

        def row_sums(c):
            nc.vector.tensor_reduce(out=log_det[:, c * TILES : (c + 1) * TILES], in_=log_s_rows(c), axis=AX.X, op=ALU.add)

        def release_gpsimd(c):
            mz = gate.tile([P, TILES, D_OUT], F32, name="mz")
            mz_t[c] = mz
            nc.vector.memset(mz[:, 0, 0:1], 0.0)

        def scale_z2(c, engine=nc.gpsimd):
            if c not in mz_t:
                mz = gate.tile([P, TILES, D_OUT], F32, name="mz")
                mz_t[c] = mz
            mz = mz_t[c]
            engine.tensor_tensor(out=mz[:], in0=z_rows(c, D_OUT), in1=ex_t[c][:], op=ALU.mult)

        def cast_z1(c, engine=nc.gpsimd):
            ot = ring4.tile([P, TILES, DIM], F32, name="ot")
            ot_t[c] = ot
            if engine is nc.scalar:
                nc.scalar.copy(out=ot[:, :, 0:D_OUT], in_=z_rows(c, 0))
                return
            nc.gpsimd.tensor_scalar(
                out=ot[:, :, 0:D_OUT],
                in0=z_rows(c, 0),
                scalar1=1.0,
                scalar2=0.0,
                op0=ALU.mult,
                op1=ALU.add,
            )

        def finish(c):
            nc.vector.tensor_tensor(out=ot_t[c][:, :, D_OUT:DIM], in0=ot_ps[c][:].rearrange("p (r d) -> p r d", d=D_OUT), in1=mz_t[c][:], op=ALU.add)
            nc.sync.dma_start(out=z_out[:, c * TILES : (c + 1) * TILES, :], in_=ot_t[c][:])

        def when(it, first, fn):
            c = (it - first) // 2
            if it >= first and (it - first) % 2 == 0 and c < N_CHUNKS:
                fn(c)

        def when_shift(it, delay, fn):
            for c in range(N_CHUNKS):
                if it == 2 * c + (6 if at_end(c) else 8) + delay:
                    fn(c)

        def copy_on_vector(copies):
            for dst, src in copies:
                nc.vector.tensor_copy(out=dst, in_=src)

        transpose_w(0)
        prep_bias(0)
        transpose_h(0)
        quantise_w(0)
        quantise_h(0, 0, 1)
        transpose_h(1)
        prep_bias(1)
        transpose_w(1)
        hidden_layer(0)
        quantise_h(0, 1, 2)
        copies = transpose_h(2, (0, 1))
        quantise_w(1)
        prep_bout()
        copy_on_vector(copies)
        hidden_layer(1)
        copies = transpose_h(3, (1,))
        quantise_h(1, 0, 1)
        copy_on_vector(copies)
        prep_wout(0)
        quantise_h(1, 1, 2)
        load(2)
        transpose_h(4)
        prep_wout(1)

        for it in range(2, N_UNITS):
            vector_copies = []
            when_shift(it, 1, add_shift_bias)
            when(it, 7, exponential)
            if it < N_UNITS:
                hidden_layer(it)
            if it + 3 < N_UNITS:
                if (it + 3) % 4 == 0 and (it + 3) // 4 + 1 < N_LOADS:
                    load((it + 3) // 4 + 1)
                vector_copies = transpose_h(it + 3, (1,) if it % 2 == 1 else ())
            when_shift(it, 1, transpose_shift)
            when(it, 4, lambda c: None if at_end(c) else scale_output(c))
            when_shift(it, 0, shift_output)
            if it % 2 == 1 and (it + 1) // 2 < N_CHUNKS:
                quantise_h((it + 1) // 2, 0, 2)
            when(it, 7, release_gpsimd)
            when(it, 7, scale_z2)
            when(it, 7, cast_z1)
            when(it, 5, lambda c: None if at_end(c) else add_scale_bias(c))
            copy_on_vector(vector_copies)
            when(it, 7, row_sums)
            when_shift(it, 1, finish)
            when(it, 2, regroup_g)
            when(it, 6, lambda c: None if at_end(c) else clamp(c))
            when(it, 2, quantise_g)
        scale_output_t(13, "tp")
        scale_output_t(14, "os")
        shift_output(12)
        shift_output(13, "tp")
        shift_output(14, "m1")
        regroup_g(15, 0, 1)
        add_scale_bias_t(13)
        add_scale_bias_t(14)
        add_shift_bias(12)
        add_shift_bias(13)
        regroup_g(15, 1, 2)
        clamp(13)
        clamp(14)
        quantise_g(15)
        transpose_scale(13)
        transpose_shift(12)
        transpose_scale(14)
        transpose_shift(13)
        exponential(13)
        exponential(14)
        scale_output_t(15, "m1")
        shift_output(15, "m1")
        add_shift_bias(14)
        add_scale_bias_t(15)
        cast_z1(13, nc.scalar)
        transpose_shift(14)
        release_gpsimd(13)
        scale_z2(13)
        finish(12)
        row_sums(14)
        clamp(15)
        transpose_scale(15)
        release_gpsimd(14)
        scale_z2(14)
        finish(13)
        row_sums(13)
        add_shift_bias(15)
        exponential(15)
        transpose_shift(15)
        cast_z1(14, nc.scalar)
        cast_z1(15, nc.scalar)
        scale_z2(15, nc.vector)
        finish(14)
        row_sums(15)
        finish(15)
        nc.sync.dma_start(out=out_1.rearrange("(p i) -> p i", i=ROWS_PP), in_=log_det[:])
